import numpy as np
import ml_dtypes


def mxq(x, axis, fmt="e4m3"):
    dtype, down = {"e4m3": (ml_dtypes.float8_e4m3fn, 7), "e5m2": (ml_dtypes.float8_e5m2, 14)}[fmt]
    v = np.moveaxis(np.asarray(x, np.float32).astype(ml_dtypes.bfloat16).astype(np.float64), axis, -1)
    blocks = v.reshape(v.shape[:-1] + (-1, 32))
    amax = np.abs(blocks).max(-1, keepdims=True)
    byte = np.maximum(np.where(amax > 0, np.frexp(amax)[1] - 1 + 127, 0) - down, 1)
    scale = np.exp2(byte - 127.0)
    codes = (blocks / scale).astype(np.float32).astype(dtype).astype(np.float64)
    return np.moveaxis((codes * scale).reshape(v.shape), -1, axis)


WIDE = False


def mx_kscale(k):
    if not WIDE:
        return np.ones(k)
    levels = np.array([18, -18])
    if k % 512:
        return np.exp2(np.random.permutation(np.resize(levels, k // 32))).repeat(32)
    a = np.empty((k // 512, 16))
    for p in range(k // 512):
        a[p, :8] = np.random.permutation(np.resize(levels, 8))
        for g in range(8):
            far = levels[np.abs(levels - a[p, g]) >= 10]
            a[p, g + 8] = far[np.random.randint(len(far))]
    return np.exp2(a.ravel()).repeat(32)


BF16 = ml_dtypes.bfloat16


def bf(x):
    return np.asarray(x, np.float32).astype(BF16)


def f64(x):
    return np.asarray(x).astype(np.float64)


B, D, H, F = 2048, 512, 1024, 512


def blend_act(v):
    t = np.tanh(v)
    return np.where(v > 0, v * 0.9 + t * 0.1, t * 0.5)


def blend_grad(v):
    t = np.tanh(v)
    d = 1.0 - t * t
    return np.where(v > 0, 0.9 + 0.1 * d, 0.5 * d)


def setup_inputs():
    s = mx_kscale(B)[:, None]
    u = mx_kscale(F)
    v = mx_kscale(H)
    x0 = bf(np.random.standard_normal((B, D)))
    W1_0 = bf(np.random.standard_normal((D, H)) / np.sqrt(D))
    b1 = bf(np.random.standard_normal(H) * 0.3)
    W2_0 = bf(np.random.standard_normal((H, F)) * 1.5 / np.sqrt(H))
    b2 = bf(np.random.standard_normal(F) * 0.3)
    g = bf(np.random.standard_normal((B, F)) * np.exp2(np.random.randint(-6, 1, (B, 1))) * 4.0 / s * u)
    z1 = f64(x0) @ f64(W1_0) + f64(b1)
    z2 = blend_act(z1) @ f64(W2_0) + f64(b2)
    return {"x": bf(f64(x0) * s),
            "W1": bf(f64(W1_0) / v),
            "b1": b1,
            "W2": bf(f64(W2_0) * v[:, None] / u),
            "b2": b2,
            "z1": np.asarray(z1, np.float32),
            "z2": np.asarray(z2, np.float32),
            "grad_out": g}


def reference(x, W1, b1, W2, b2, z1, z2, grad_out):
    dz2 = np.where(f64(z2) > 0, f64(grad_out), 0.0)
    dh = mxq(dz2, 1, "e5m2") @ mxq(f64(W2), 1, "e4m3").T
    dz1 = dh * blend_grad(f64(z1))
    dx = mxq(dz1, 1, "e5m2") @ mxq(f64(W1), 1, "e4m3").T
    dW1 = mxq(f64(x), 0, "e4m3").T @ mxq(dz1, 0, "e5m2")
    return dx, dW1

@@ -1,0 +1,417 @@
+import math
+from contextlib import ExitStack
+
+import concourse.mybir as mybir
+from concourse.masks import make_identity
+
+FLOPS = 3 * 2 * 2048 * 512 * 1024
+BYTES = 2048 * 512 * 2 * 2 + 512 * 1024 * 2 * 2 + 2048 * 1024 * 4 + 2048 * 512 * 4 + 2048 * 512 * 4 + 512 * 1024 * 4
+
+F32 = mybir.dt.float32
+BF16 = mybir.dt.bfloat16
+U32 = mybir.dt.uint32
+U8 = mybir.dt.uint8
+E4M3 = mybir.dt.float8_e4m3fn_x4
+E5M2 = mybir.dt.float8_e5m2_x4
+ALU = mybir.AluOpType
+ACT = mybir.ActivationFunctionType
+
+P = 128
+J = 4
+GROUPS = 4
+HALVES = 2
+W = 512
+C_SQ = math.sqrt(0.4)
+VIA_PE = ()
+G_COLS = 384
+G_STEP = 192
+XPE = True
+BANKS = {"tr": 2, "acc": 4, "dhb": 2}
+
+
+def tile_complexnn_pa_v_kernel(tc, x, W1, b1, W2, b2, z1, z2, grad_out, out_0, out_1):
+    nc = tc.nc
+    with ExitStack() as ctx:
+        keep = ctx.enter_context(tc.tile_pool(name="keep", bufs=1))
+        zin = ctx.enter_context(tc.tile_pool(name="zin", bufs=4))
+        gin = ctx.enter_context(tc.tile_pool(name="gin", bufs=2))
+        trio = ctx.enter_context(tc.tile_pool(name="trio", bufs=3))
+        work = ctx.enter_context(tc.tile_pool(name="work", bufs=3))
+        pair = ctx.enter_context(tc.tile_pool(name="pair", bufs=2))
+        psum = ctx.enter_context(tc.psum_pool(name="psum", bufs=2))
+
+        ident = keep.tile([P, P], F32, name="ident")
+        make_identity(nc, ident[:])
+        ident_bf = keep.tile([P, P], BF16, name="ident_bf")
+        nc.vector.tensor_copy(out=ident_bf[:], in_=ident[:])
+        warm = keep.tile([P, 8], F32, name="warm")
+        nc.vector.memset(warm[:], 0.0)
+        warm_out = keep.tile([P, 8], F32, name="warm_out")
+        nc.scalar.activation(out=warm_out[:], in_=warm[:], func=ACT.Tanh)
+
+        z1t, z2t, gt, xt_raw = {}, {}, {}, {}
+        w1_raw, w2_raw = {}, {}
+        w1_codes = [keep.tile([P, W], U32, name="w1_codes%d" % i, align_bytes=64) for i in range(HALVES)]
+        w1_scale = [keep.tile([P, W], U8, name="w1_scale%d" % i, align_bytes=64) for i in range(HALVES)]
+        w2_codes = [keep.tile([P, W], U32, name="w2_codes%d" % i, align_bytes=64) for i in range(HALVES)]
+        w2_scale = [keep.tile([P, W], U8, name="w2_scale%d" % i, align_bytes=64) for i in range(HALVES)]
+        g_codes = [keep.tile([P, W], U32, name="g_codes%d" % g, align_bytes=64) for g in range(GROUPS)]
+        g_scale = [keep.tile([P, W], U8, name="g_scale%d" % g, align_bytes=64) for g in range(GROUPS)]
+        x_codes = [keep.tile([P, W], U32, name="x_codes%d" % g, align_bytes=64) for g in range(GROUPS)]
+        x_scale = [keep.tile([P, W], U8, name="x_scale%d" % g, align_bytes=64) for g in range(GROUPS)]
+        f_codes = [keep.tile([P, W], U32, name="f_codes%d" % c, align_bytes=64) for c in range(4)]
+        f_scale = [keep.tile([P, W], U8, name="f_scale%d" % c, align_bytes=64) for c in range(4)]
+        t_codes = [keep.tile([P, W], U32, name="t_codes%d" % c, align_bytes=64) for c in range(8)]
+        t_scale = [keep.tile([P, W], U8, name="t_scale%d" % c, align_bytes=64) for c in range(8)]
+
+        def rows(dram, g):
+            return dram[g * W : (g + 1) * W, :].rearrange("(p j) w -> p j w", j=J)
+
+        def new_bank(tag, shape=(P, W)):
+            return psum.tile(list(shape), F32, name=tag, tag=tag, bufs=BANKS[tag])
+
+        def load_z1(c, j0=0, j1=J):
+            if c not in z1t:
+                z1t[c] = zin.tile([P, J, W], F32, name="z1c")
+            h0 = (c // 4) * W
+            src = rows(z1, c % 4)
+            nc.sync.dma_start(out=z1t[c][:, j0:j1, :], in_=src[:, j0:j1, h0 : h0 + W])
+
+        def load_g(g, j0=0, j1=J):
+            if g not in z2t:
+                z2t[g] = gin.tile([P, J, W], F32, name="z2g")
+                gt[g] = trio.tile([P, J, W], BF16, name="gg")
+            nc.sync.dma_start(out=z2t[g][:, j0:j1, :], in_=rows(z2, g)[:, j0:j1, :])
+            nc.sync.dma_start(out=gt[g][:, j0:j1, :], in_=rows(grad_out, g)[:, j0:j1, :])
+
+        def load_w2(hh):
+            w2_raw[hh] = pair.tile([P, 4, W], BF16, name="w_raw", tag="w_raw")
+            nc.sync.dma_start(out=w2_raw[hh][:], in_=W2[hh * W : (hh + 1) * W, :].rearrange("(i p) f -> p i f", p=P))
+
+        def load_w1(hh):
+            w1_raw[hh] = pair.tile([P, 4, W], BF16, name="w_raw", tag="w_raw")
+            nc.sync.dma_start(out=w1_raw[hh][:], in_=W1[:, hh * W : (hh + 1) * W].rearrange("(i p) h -> p i h", p=P))
+
+        def load_x(g):
+            xt_raw[g] = pair.tile([P, J, W], BF16, name="x_raw")
+            nc.sync.dma_start(out=xt_raw[g][:], in_=rows(x, g))
+
+        def transposes(src, blocks, tag):
+            banks = []
+            for q in range(0, blocks, 2):
+                bank = new_bank(tag, [P, 2, 2, P])
+                for b in range(2):
+                    for u in range(2):
+                        nc.tensor.transpose(bank[:, b, u, :], src[:, q + b, u:256:2], ident[:])
+                banks.append(bank)
+            return banks
+
+        def evacuate(banks, grouped, engines, block0=0):
+            dst = grouped[:].bitcast(F32)
+            for q, bank in enumerate(banks):
+                out = dst[:, block0 + 2 * q : block0 + 2 * q + 2, :, :]
+                in_ = bank[:].rearrange("p b u r -> p b r u")
+                if engines[q] == "s":
+                    nc.scalar.copy(out=out, in_=in_)
+                else:
+                    nc.vector.tensor_copy(out=out, in_=in_)
+
+        def quantize(grouped, codes, scale, fmt, c0=0, c1=W):
+            nc.vector.quantize_mx(out=codes[:, c0:c1].bitcast(fmt), scales=scale[:, c0:c1], in_=grouped[:, 4 * c0 : 4 * c1])
+
+        def k_last_tile(tag):
+            return trio.tile([P, 4, P, 4], BF16, name="kg", tag="kg", align_bytes=64)
+
+        def flat4(t):
+            return t[:].rearrange("p b r k -> p (b r k)")
+
+        dz2t, dz2g = {}, {}
+
+        def mask_dz2(g, j0=0, j1=J):
+            dz2t[g] = gt[g]
+            nc.vector.scalar_tensor_tensor(
+                out=dz2t[g][:, j0:j1, :], in0=z2t[g][:, j0:j1, :], scalar=0.0, in1=gt[g][:, j0:j1, :], op0=ALU.is_gt, op1=ALU.mult)
+
+        tt, nt = {}, {}
+
+        def tanh(c, j0=0, j1=J):
+            if c not in tt:
+                tt[c] = work.tile([P, J, W], F32, name="th")
+            nc.scalar.activation(out=tt[c][:, j0:j1, :], in_=z1t[c][:, j0:j1, :], func=ACT.Tanh)
+
+        def square(c, j0=0, j1=J):
+            nc.scalar.activation(out=tt[c][:, j0:j1, :], in_=tt[c][:, j0:j1, :], func=ACT.Square, scale=C_SQ)
+
+        def side(c, j0=0, j1=J):
+            if c not in nt:
+                nt[c] = pair.tile([P, J, W], BF16, name="side")
+            nc.vector.tensor_scalar(
+                out=nt[c][:, j0:j1, :], in0=z1t[c][:, j0:j1, :], scalar1=0.0, scalar2=1.25, op0=ALU.is_gt, op1=ALU.subtract)
+
+        def slope(c, j0=0, j1=J):
+            nc.vector.scalar_tensor_tensor(
+                out=tt[c][:, j0:j1, :], in0=tt[c][:, j0:j1, :], scalar=0.5, in1=nt[c][:, j0:j1, :], op0=ALU.add, op1=ALU.mult)
+
+        dz1t, dhb = {}, {}
+
+        def dh(c, j):
+            bank = new_bank("dhb")
+            g, hh = c % 4, c // 4
+            nc.tensor.matmul_mx(
+                out=bank[:], lhsT=g_codes[g][:, j * P : (j + 1) * P].bitcast(E5M2), lhsT_scale=g_scale[g][:, j * P : (j + 1) * P],
+                rhs=w2_codes[hh][:].bitcast(E4M3), rhs_scale=w2_scale[hh][:], start=True, stop=True)
+            dhb[c, j] = bank
+
+        def final(c, j):
+            if c not in dz1t:
+                dz1t[c] = pair.tile([P, J, W], BF16, name="dz1")
+            nc.vector.scalar_tensor_tensor(
+                out=dz1t[c][:, j, :], in0=tt[c][:, j, :], scalar=1.125, in1=dhb[c, j][:], op0=ALU.add, op1=ALU.mult)
+
+        def interleave(src, name, engine):
+            t = trio.tile([P, W, J], BF16, name="ig", tag="ig", align_bytes=64)
+            out, in_ = t[:], src[:].rearrange("p j w -> p w j")
+            if engine == "s":
+                nc.scalar.copy(out=out, in_=in_)
+            else:
+                nc.vector.tensor_copy(out=out, in_=in_)
+            return t
+
+        def interleave_pe(src, tag):
+            t = trio.tile([P, W, J], BF16, name="ig", tag="ig", align_bytes=64)
+            for q in range(2):
+                bank = psum.tile([P, 256, J], BF16, name=tag, tag=tag, bufs=BANKS[tag])
+                for r in range(2):
+                    h0 = 256 * q + 128 * r
+                    nc.tensor.matmul(out=bank[:, 128 * r : 128 * (r + 1), :], lhsT=ident_bf[:], rhs=src[:, :, h0 : h0 + 128].rearrange("p j h -> p h j"), start=True, stop=True)
+                nc.scalar.copy(out=t[:, 256 * q : 256 * (q + 1), :], in_=bank[:])
+            return t
+
+        def flat_t(t):
+            return t[:].rearrange("p w j -> p (w j)")
+
+        outs = {}
+
+        def dx(c, j, tag):
+            bank = new_bank(tag)
+            for hh in range(HALVES):
+                cc = hh * 4 + c % 4
+                nc.tensor.matmul_mx(
+                    out=bank[:], lhsT=f_codes[cc][:, j * P : (j + 1) * P].bitcast(E5M2), lhsT_scale=f_scale[cc][:, j * P : (j + 1) * P],
+                    rhs=w1_codes[hh][:].bitcast(E4M3), rhs_scale=w1_scale[hh][:], start=(hh == 0), stop=(hh == 1))
+            return bank
+
+        def copy_out(dst, bank, engine):
+            if engine == "s":
+                nc.scalar.copy(out=dst, in_=bank[:])
+            else:
+                nc.vector.tensor_copy(out=dst, in_=bank[:])
+
+        def dw_pass(bank, i, hh, g):
+            c = hh * 4 + g
+            nc.tensor.matmul_mx(
+                out=bank[:], lhsT=x_codes[g][:, i * P : (i + 1) * P].bitcast(E4M3), lhsT_scale=x_scale[g][:, i * P : (i + 1) * P],
+                rhs=t_codes[c][:].bitcast(E5M2), rhs_scale=t_scale[c][:], start=(g == 0), stop=(g == 3))
+
+        def store_dw(bank, i, hh, engine):
+            t = work.tile([P, W], F32, name="dw_out", bufs=5)
+            copy_out(t[:], bank, engine)
+            nc.sync.dma_start(out=out_1[i * P : (i + 1) * P, hh * W : (hh + 1) * W], in_=t[:])
+
+        def store_dx(c, j0, j1):
+            nc.sync.dma_start(out=rows(out_0, c % 4)[:, j0:j1, :], in_=outs[c, j0][:])
+
+        def dz2_chain(g, j0=0, j1=J, tag="acc"):
+            mask_dz2(g, j0, j1)
+            flip_z(g, j0, j1, tag)
+
+        def flip_z(g, j0=0, j1=J, tag="acc"):
+            if g not in dz2g:
+                dz2g[g] = k_last_tile("kg")
+            evacuate(transposes(dz2t[g][:, j0:j1, :].bitcast(F32), j1 - j0, tag), dz2g[g], "ss", j0)
+
+        def quant_z(g):
+            quantize(flat4(dz2g[g]), g_codes[g], g_scale[g], E5M2)
+
+        fgt, tgt, xg = {}, {}, {}
+
+        def quant_f(c, c0=0, c1=W):
+            if c >= 4 and len(f_codes) <= c:
+                f_codes.append(pair.tile([P, W], U32, name="f_codes_b", align_bytes=64))
+                f_scale.append(pair.tile([P, W], U8, name="f_scale_b", align_bytes=64))
+            quantize(flat4(fgt[c]), f_codes[c], f_scale[c], E5M2, c0, c1)
+
+        def quant_t(c):
+            quantize(flat_t(tgt[c]), t_codes[c], t_scale[c], E5M2)
+
+        def flip(c):
+            fgt[c] = k_last_tile("fg")
+            evacuate(transposes(dz1t[c][:].bitcast(F32), 4, "tr"), fgt[c], "ss")
+
+        def weave(c):
+            tgt[c] = interleave_pe(dz1t[c], "acc") if c in VIA_PE else interleave(dz1t[c], "tg", "v")
+
+        def weave_g(c):
+            tgt[c] = keep.tile([P, W, J], BF16, name="tg", tag="tg", align_bytes=64)
+            for h0 in range(0, G_COLS, G_STEP):
+                nc.gpsimd.tensor_scalar(
+                    out=tgt[c][:, h0 : h0 + G_STEP, :], in0=dz1t[c][:, :, h0 : h0 + G_STEP].rearrange("p j h -> p h j"),
+                    scalar1=1.0, scalar2=0.0, op0=ALU.mult, op1=ALU.add)
+
+        def weave_v(c):
+            nc.vector.tensor_copy(out=tgt[c][:, G_COLS:, :], in_=dz1t[c][:, :, G_COLS:].rearrange("p j h -> p h j"))
+
+        def weave_x(g):
+            xg[g] = interleave_pe(xt_raw[g], "acc") if XPE else interleave(xt_raw[g], "xg", "s")
+
+        def quant_x(g):
+            quantize(flat_t(xg[g]), x_codes[g], x_scale[g], E4M3)
+
+        wg = {}
+
+        def flip_w(name, raw, tag="acc"):
+            wg[name] = k_last_tile("kg")
+            evacuate(transposes(raw[:].bitcast(F32), 4, tag), wg[name], "ss")
+
+        def quant_w(name, codes, scale):
+            quantize(flat4(wg[name]), codes, scale, E4M3)
+
+        def dx_tiles(c, js, tag, engines):
+            for j in js:
+                if j % 2 == 0:
+                    outs[c, j] = trio.tile([P, 2, W], F32, name="dx_out")
+                bank = dx(c, j, tag)
+                copy_out(outs[c, j - j % 2][:, j % 2, :], bank, engines[j % 2])
+                if j % 2 == 1:
+                    store_dx(c, j - 1, j + 1)
+
+        dwb = {}
+
+        def dw_all(tiles):
+            for i in tiles:
+                bank = new_bank("acc")
+                for gg in range(GROUPS):
+                    dw_pass(bank, i, 0, gg)
+                store_dw(bank, i, 0, "s")
+
+        with tc.manual_schedule():
+            load_g(0, 0, 2)
+            load_w2(0)
+            load_z1(0, 0, 2)
+            load_g(0, 2, 4)
+            load_z1(0, 2, 4)
+            load_z1(1)
+            load_g(1)
+            load_z1(2)
+            load_w2(1)
+
+            dz2_chain(0, 0, 2)
+            flip_w("w20", w2_raw[0], "tr")
+            tanh(0, 0, 2)
+            square(0, 0, 2)
+            side(0, 0, 2)
+            quant_w("w20", w2_codes[0], w2_scale[0])
+            dz2_chain(0, 2, 4)
+            load_g(2)
+            load_z1(3)
+            load_x(0)
+            tanh(0, 2, 4)
+            square(0, 2, 4)
+            slope(0, 0, 2)
+            side(0, 2, 4)
+            quant_z(0)
+            tanh(1)
+            for j in range(J):
+                dh(0, j)
+                if j == 2:
+                    slope(0, 2, 4)
+                final(0, j)
+            square(1)
+            flip(0)
+            mask_dz2(1)
+            load_g(3)
+            load_x(1)
+            load_z1(4)
+            side(1)
+            flip_z(1)
+            tanh(2)
+            slope(1)
+            quant_z(1)
+            dh(1, 0)
+            dh(1, 1)
+            square(2)
+            mask_dz2(2)
+            flip_z(2)
+            side(2)
+            for c in range(1, 8):
+                if c > 1:
+                    quant_t(c - 2)
+                quant_f(c - 1)
+                weave_g(c - 1)
+                if c < 6:
+                    tanh(c + 2)
+                for j in range(J):
+                    if c > 4 and j > 0:
+                        dx_tiles(c - 1, (j - 1,), "acc", "ss")
+                    if j > 1:
+                        dh(c, j)
+                    final(c, j)
+                if c > 4:
+                    dx_tiles(c - 1, (3,), "acc", "ss")
+                if c == 7:
+                    for i in range(4):
+                        dwb[i] = new_bank("acc")
+                        dw_pass(dwb[i], i, 1, 0)
+                        dw_pass(dwb[i], i, 1, 1)
+                flip(c)
+                if c in (2, 3, 4, 5):
+                    quant_x(c - 2)
+                weave_v(c - 1)
+                if c + 1 < 4:
+                    quant_z(c + 1)
+                if c == 3:
+                    quant_w("w21", w2_codes[1], w2_scale[1])
+                if c < 7:
+                    dh(c + 1, 0)
+                    dh(c + 1, 1)
+                if c + 2 < 4:
+                    mask_dz2(c + 2)
+                if c < 7:
+                    slope(c + 1)
+                if c == 5:
+                    dw_all((0, 1))
+                if c == 6:
+                    dw_all((2, 3))
+                if c < 6:
+                    square(c + 2)
+                if c + 2 < 4:
+                    flip_z(c + 2)
+                if c in (3, 4):
+                    quant_w("w1%d" % (c - 3), w1_codes[c - 3], w1_scale[c - 3])
+                if c < 6:
+                    side(c + 2)
+                if c in (1, 2, 3, 4):
+                    weave_x(c - 1)
+                if c + 4 < 8:
+                    load_z1(c + 4)
+                if c == 1:
+                    flip_w("w21", w2_raw[1])
+                    load_x(2)
+                    load_w1(0)
+                if c == 2:
+                    load_x(3)
+                    load_w1(1)
+                if c in (2, 3):
+                    flip_w("w1%d" % (c - 2), w1_raw[c - 2])
+            tgt[7] = interleave(dz1t[7], "tg", "v")
+            quant_t(6)
+            quant_f(7, 0, 256)
+            quant_t(7)
+            quant_f(7, 256, 512)
+            for i in range(4):
+                dw_pass(dwb[i], i, 1, 2)
+            dx_tiles(7, (0, 1), "tr", "vs")
+            for i in range(4):
+                dw_pass(dwb[i], i, 1, 3)
+                store_dw(dwb[i], i, 1, "vs"[i % 2])
+            dx_tiles(7, (2, 3), "dhb", "vs")

@@ -18,14 +18,9 @@ ACT = mybir.ActivationFunctionType
 
 P = 128
 J = 4
-GROUPS = 4
-HALVES = 2
 W = 512
 C_SQ = math.sqrt(0.4)
-VIA_PE = ()
-G_COLS = 384
-G_STEP = 192
-XPE = True
+G_COLS = 352
 BANKS = {"tr": 2, "acc": 4, "dhb": 2}
 
 
@@ -34,10 +29,9 @@ def tile_complexnn_pa_v_kernel(tc, x, W1, b1, W2, b2, z1, z2, grad_out, out_0, o
     with ExitStack() as ctx:
         keep = ctx.enter_context(tc.tile_pool(name="keep", bufs=1))
         zin = ctx.enter_context(tc.tile_pool(name="zin", bufs=4))
-        gin = ctx.enter_context(tc.tile_pool(name="gin", bufs=2))
-        trio = ctx.enter_context(tc.tile_pool(name="trio", bufs=3))
-        work = ctx.enter_context(tc.tile_pool(name="work", bufs=3))
         pair = ctx.enter_context(tc.tile_pool(name="pair", bufs=2))
+        trio = ctx.enter_context(tc.tile_pool(name="trio", bufs=3))
+        quad = ctx.enter_context(tc.tile_pool(name="quad", bufs=4))
         psum = ctx.enter_context(tc.psum_pool(name="psum", bufs=2))
 
         ident = keep.tile([P, P], F32, name="ident")
@@ -49,94 +43,93 @@ def tile_complexnn_pa_v_kernel(tc, x, W1, b1, W2, b2, z1, z2, grad_out, out_0, o
         warm_out = keep.tile([P, 8], F32, name="warm_out")
         nc.scalar.activation(out=warm_out[:], in_=warm[:], func=ACT.Tanh)
 
-        z1t, z2t, gt, xt_raw = {}, {}, {}, {}
-        w1_raw, w2_raw = {}, {}
-        w1_codes = [keep.tile([P, W], U32, name="w1_codes%d" % i, align_bytes=64) for i in range(HALVES)]
-        w1_scale = [keep.tile([P, W], U8, name="w1_scale%d" % i, align_bytes=64) for i in range(HALVES)]
-        w2_codes = [keep.tile([P, W], U32, name="w2_codes%d" % i, align_bytes=64) for i in range(HALVES)]
-        w2_scale = [keep.tile([P, W], U8, name="w2_scale%d" % i, align_bytes=64) for i in range(HALVES)]
-        g_codes = [keep.tile([P, W], U32, name="g_codes%d" % g, align_bytes=64) for g in range(GROUPS)]
-        g_scale = [keep.tile([P, W], U8, name="g_scale%d" % g, align_bytes=64) for g in range(GROUPS)]
-        x_codes = [keep.tile([P, W], U32, name="x_codes%d" % g, align_bytes=64) for g in range(GROUPS)]
-        x_scale = [keep.tile([P, W], U8, name="x_scale%d" % g, align_bytes=64) for g in range(GROUPS)]
-        f_codes = [keep.tile([P, W], U32, name="f_codes%d" % c, align_bytes=64) for c in range(4)]
-        f_scale = [keep.tile([P, W], U8, name="f_scale%d" % c, align_bytes=64) for c in range(4)]
-        t_codes = [keep.tile([P, W], U32, name="t_codes%d" % c, align_bytes=64) for c in range(8)]
-        t_scale = [keep.tile([P, W], U8, name="t_scale%d" % c, align_bytes=64) for c in range(8)]
+        def codes_pair(name):
+            return (keep.tile([P, W], U32, name="c_" + name, align_bytes=64), keep.tile([P, W], U8, name="s_" + name, align_bytes=64))
+
+        wq = {n: codes_pair(n) for n in ("w20", "w21", "w10", "w11")}
+        zq = [codes_pair("z%d" % g) for g in range(4)]
+        xq = [codes_pair("x%d" % g) for g in range(4)]
+        tq = [codes_pair("t%d" % c) for c in range(8)]
+        fq = {c: codes_pair("f%d" % c) for c in range(4)}
+        bank, z1t, z2t, gt, x_raw, w_raw, kg, ig, tt, nt, dz1t, outs = {}, {}, {}, {}, {}, {}, {}, {}, {}, {}, {}, {}
 
         def rows(dram, g):
             return dram[g * W : (g + 1) * W, :].rearrange("(p j) w -> p j w", j=J)
 
-        def new_bank(tag, shape=(P, W)):
-            return psum.tile(list(shape), F32, name=tag, tag=tag, bufs=BANKS[tag])
+        def new_bank(tag, shape=(P, W), dtype=F32):
+            return psum.tile(list(shape), dtype, name=tag, tag=tag, bufs=BANKS[tag])
 
         def load_z1(c, j0=0, j1=J):
             if c not in z1t:
                 z1t[c] = zin.tile([P, J, W], F32, name="z1c")
             h0 = (c // 4) * W
-            src = rows(z1, c % 4)
-            nc.sync.dma_start(out=z1t[c][:, j0:j1, :], in_=src[:, j0:j1, h0 : h0 + W])
+            nc.sync.dma_start(out=z1t[c][:, j0:j1, :], in_=rows(z1, c % 4)[:, j0:j1, h0 : h0 + W])
 
         def load_g(g, j0=0, j1=J):
             if g not in z2t:
-                z2t[g] = gin.tile([P, J, W], F32, name="z2g")
+                z2t[g] = pair.tile([P, J, W], F32, name="z2g")
                 gt[g] = trio.tile([P, J, W], BF16, name="gg")
             nc.sync.dma_start(out=z2t[g][:, j0:j1, :], in_=rows(z2, g)[:, j0:j1, :])
             nc.sync.dma_start(out=gt[g][:, j0:j1, :], in_=rows(grad_out, g)[:, j0:j1, :])
 
-        def load_w2(hh):
-            w2_raw[hh] = pair.tile([P, 4, W], BF16, name="w_raw", tag="w_raw")
-            nc.sync.dma_start(out=w2_raw[hh][:], in_=W2[hh * W : (hh + 1) * W, :].rearrange("(i p) f -> p i f", p=P))
-
-        def load_w1(hh):
-            w1_raw[hh] = pair.tile([P, 4, W], BF16, name="w_raw", tag="w_raw")
-            nc.sync.dma_start(out=w1_raw[hh][:], in_=W1[:, hh * W : (hh + 1) * W].rearrange("(i p) h -> p i h", p=P))
+        def load_w(n):
+            w_raw[n] = pair.tile([P, 4, W], BF16, name="w_raw", tag="w_raw")
+            h0 = int(n[2]) * W
+            src = W2[h0 : h0 + W, :] if n[1] == "2" else W1[:, h0 : h0 + W]
+            nc.sync.dma_start(out=w_raw[n][:], in_=src.rearrange("(i p) f -> p i f", p=P))
 
         def load_x(g):
-            xt_raw[g] = pair.tile([P, J, W], BF16, name="x_raw")
-            nc.sync.dma_start(out=xt_raw[g][:], in_=rows(x, g))
+            x_raw[g] = pair.tile([P, J, W], BF16, name="x_raw")
+            nc.sync.dma_start(out=x_raw[g][:], in_=rows(x, g))
 
-        def transposes(src, blocks, tag):
-            banks = []
-            for q in range(0, blocks, 2):
-                bank = new_bank(tag, [P, 2, 2, P])
-                for b in range(2):
-                    for u in range(2):
-                        nc.tensor.transpose(bank[:, b, u, :], src[:, q + b, u:256:2], ident[:])
-                banks.append(bank)
-            return banks
+        def turn(key, src, q, tag):
+            bank[key, q] = new_bank(tag, [P, 2, 2, P])
+            words = src[:].bitcast(F32)
+            for b in range(2):
+                for u in range(2):
+                    nc.tensor.transpose(bank[key, q][:, b, u, :], words[:, 2 * q + b, u:256:2], ident[:])
 
-        def evacuate(banks, grouped, engines, block0=0):
-            dst = grouped[:].bitcast(F32)
-            for q, bank in enumerate(banks):
-                out = dst[:, block0 + 2 * q : block0 + 2 * q + 2, :, :]
-                in_ = bank[:].rearrange("p b u r -> p b r u")
-                if engines[q] == "s":
-                    nc.scalar.copy(out=out, in_=in_)
-                else:
-                    nc.vector.tensor_copy(out=out, in_=in_)
+        def take(key, q, engine="s"):
+            if key not in kg:
+                kg[key] = quad.tile([P, 4, P, 4], BF16, name="kg", tag="kg", align_bytes=64)
+            out = kg[key][:].bitcast(F32)[:, 2 * q : 2 * q + 2, :, :]
+            in_ = bank[key, q][:].rearrange("p b u r -> p b r u")
+            if engine == "s":
+                nc.scalar.copy(out=out, in_=in_)
+            else:
+                nc.vector.tensor_copy(out=out, in_=in_)
 
-        def quantize(grouped, codes, scale, fmt, c0=0, c1=W):
-            nc.vector.quantize_mx(out=codes[:, c0:c1].bitcast(fmt), scales=scale[:, c0:c1], in_=grouped[:, 4 * c0 : 4 * c1])
+        def quantize(flat, dst, fmt, c0=0, c1=W):
+            nc.vector.quantize_mx(out=dst[0][:, c0:c1].bitcast(fmt), scales=dst[1][:, c0:c1], in_=flat[:, 4 * c0 : 4 * c1])
 
-        def k_last_tile(tag):
-            return trio.tile([P, 4, P, 4], BF16, name="kg", tag="kg", align_bytes=64)
+        def flat_k(key):
+            return kg[key][:].rearrange("p b r k -> p (b r k)")
 
-        def flat4(t):
-            return t[:].rearrange("p b r k -> p (b r k)")
+        def turn_w(n, q, tag="acc"):
+            turn(n, w_raw[n], q, tag)
 
-        dz2t, dz2g = {}, {}
+        def take_w(n, q, engine="s"):
+            take(n, q, engine)
 
-        def mask_dz2(g, j0=0, j1=J):
-            dz2t[g] = gt[g]
+        def quant_w(n):
+            quantize(flat_k(n), wq[n], E4M3)
+
+        def mask(g, j0=0, j1=J):
             nc.vector.scalar_tensor_tensor(
-                out=dz2t[g][:, j0:j1, :], in0=z2t[g][:, j0:j1, :], scalar=0.0, in1=gt[g][:, j0:j1, :], op0=ALU.is_gt, op1=ALU.mult)
+                out=gt[g][:, j0:j1, :], in0=z2t[g][:, j0:j1, :], scalar=0.0, in1=gt[g][:, j0:j1, :], op0=ALU.is_gt, op1=ALU.mult)
 
-        tt, nt = {}, {}
+        def turn_z(g, q):
+            turn(("z", g), gt[g], q, "acc")
+
+        def take_z(g, q):
+            take(("z", g), q)
+
+        def quant_z(g, c0=0, c1=W):
+            quantize(flat_k(("z", g)), zq[g], E5M2, c0, c1)
 
         def tanh(c, j0=0, j1=J):
             if c not in tt:
-                tt[c] = work.tile([P, J, W], F32, name="th")
+                tt[c] = trio.tile([P, J, W], F32, name="th")
             nc.scalar.activation(out=tt[c][:, j0:j1, :], in_=z1t[c][:, j0:j1, :], func=ACT.Tanh)
 
         def square(c, j0=0, j1=J):
@@ -152,266 +145,443 @@ def tile_complexnn_pa_v_kernel(tc, x, W1, b1, W2, b2, z1, z2, grad_out, out_0, o
             nc.vector.scalar_tensor_tensor(
                 out=tt[c][:, j0:j1, :], in0=tt[c][:, j0:j1, :], scalar=0.5, in1=nt[c][:, j0:j1, :], op0=ALU.add, op1=ALU.mult)
 
-        dz1t, dhb = {}, {}
-
         def dh(c, j):
-            bank = new_bank("dhb")
-            g, hh = c % 4, c // 4
+            bank["dh", c, j] = new_bank("dhb")
+            z, w = zq[c % 4], wq["w2%d" % (c // 4)]
+            cols = slice(j * P, (j + 1) * P)
             nc.tensor.matmul_mx(
-                out=bank[:], lhsT=g_codes[g][:, j * P : (j + 1) * P].bitcast(E5M2), lhsT_scale=g_scale[g][:, j * P : (j + 1) * P],
-                rhs=w2_codes[hh][:].bitcast(E4M3), rhs_scale=w2_scale[hh][:], start=True, stop=True)
-            dhb[c, j] = bank
+                out=bank["dh", c, j][:], lhsT=z[0][:, cols].bitcast(E5M2), lhsT_scale=z[1][:, cols],
+                rhs=w[0][:].bitcast(E4M3), rhs_scale=w[1][:], start=True, stop=True)
 
         def final(c, j):
             if c not in dz1t:
                 dz1t[c] = pair.tile([P, J, W], BF16, name="dz1")
             nc.vector.scalar_tensor_tensor(
-                out=dz1t[c][:, j, :], in0=tt[c][:, j, :], scalar=1.125, in1=dhb[c, j][:], op0=ALU.add, op1=ALU.mult)
+                out=dz1t[c][:, j, :], in0=tt[c][:, j, :], scalar=1.125, in1=bank["dh", c, j][:], op0=ALU.add, op1=ALU.mult)
 
-        def interleave(src, name, engine):
-            t = trio.tile([P, W, J], BF16, name="ig", tag="ig", align_bytes=64)
-            out, in_ = t[:], src[:].rearrange("p j w -> p w j")
-            if engine == "s":
-                nc.scalar.copy(out=out, in_=in_)
-            else:
-                nc.vector.tensor_copy(out=out, in_=in_)
-            return t
+        def turn_f(c, q):
+            turn(("f", c), dz1t[c], q, "tr")
 
-        def interleave_pe(src, tag):
-            t = trio.tile([P, W, J], BF16, name="ig", tag="ig", align_bytes=64)
-            for q in range(2):
-                bank = psum.tile([P, 256, J], BF16, name=tag, tag=tag, bufs=BANKS[tag])
-                for r in range(2):
-                    h0 = 256 * q + 128 * r
-                    nc.tensor.matmul(out=bank[:, 128 * r : 128 * (r + 1), :], lhsT=ident_bf[:], rhs=src[:, :, h0 : h0 + 128].rearrange("p j h -> p h j"), start=True, stop=True)
-                nc.scalar.copy(out=t[:, 256 * q : 256 * (q + 1), :], in_=bank[:])
-            return t
-
-        def flat_t(t):
-            return t[:].rearrange("p w j -> p (w j)")
-
-        outs = {}
-
-        def dx(c, j, tag):
-            bank = new_bank(tag)
-            for hh in range(HALVES):
-                cc = hh * 4 + c % 4
-                nc.tensor.matmul_mx(
-                    out=bank[:], lhsT=f_codes[cc][:, j * P : (j + 1) * P].bitcast(E5M2), lhsT_scale=f_scale[cc][:, j * P : (j + 1) * P],
-                    rhs=w1_codes[hh][:].bitcast(E4M3), rhs_scale=w1_scale[hh][:], start=(hh == 0), stop=(hh == 1))
-            return bank
-
-        def copy_out(dst, bank, engine):
-            if engine == "s":
-                nc.scalar.copy(out=dst, in_=bank[:])
-            else:
-                nc.vector.tensor_copy(out=dst, in_=bank[:])
-
-        def dw_pass(bank, i, hh, g):
-            c = hh * 4 + g
-            nc.tensor.matmul_mx(
-                out=bank[:], lhsT=x_codes[g][:, i * P : (i + 1) * P].bitcast(E4M3), lhsT_scale=x_scale[g][:, i * P : (i + 1) * P],
-                rhs=t_codes[c][:].bitcast(E5M2), rhs_scale=t_scale[c][:], start=(g == 0), stop=(g == 3))
-
-        def store_dw(bank, i, hh, engine):
-            t = work.tile([P, W], F32, name="dw_out", bufs=5)
-            copy_out(t[:], bank, engine)
-            nc.sync.dma_start(out=out_1[i * P : (i + 1) * P, hh * W : (hh + 1) * W], in_=t[:])
-
-        def store_dx(c, j0, j1):
-            nc.sync.dma_start(out=rows(out_0, c % 4)[:, j0:j1, :], in_=outs[c, j0][:])
-
-        def dz2_chain(g, j0=0, j1=J, tag="acc"):
-            mask_dz2(g, j0, j1)
-            flip_z(g, j0, j1, tag)
-
-        def flip_z(g, j0=0, j1=J, tag="acc"):
-            if g not in dz2g:
-                dz2g[g] = k_last_tile("kg")
-            evacuate(transposes(dz2t[g][:, j0:j1, :].bitcast(F32), j1 - j0, tag), dz2g[g], "ss", j0)
-
-        def quant_z(g):
-            quantize(flat4(dz2g[g]), g_codes[g], g_scale[g], E5M2)
-
-        fgt, tgt, xg = {}, {}, {}
+        def take_f(c, q):
+            take(("f", c), q)
 
         def quant_f(c, c0=0, c1=W):
-            if c >= 4 and len(f_codes) <= c:
-                f_codes.append(pair.tile([P, W], U32, name="f_codes_b", align_bytes=64))
-                f_scale.append(pair.tile([P, W], U8, name="f_scale_b", align_bytes=64))
-            quantize(flat4(fgt[c]), f_codes[c], f_scale[c], E5M2, c0, c1)
+            if c not in fq:
+                fq[c] = (pair.tile([P, W], U32, name="c_f", align_bytes=64), pair.tile([P, W], U8, name="s_f", align_bytes=64))
+            quantize(flat_k(("f", c)), fq[c], E5M2, c0, c1)
 
-        def quant_t(c):
-            quantize(flat_t(tgt[c]), t_codes[c], t_scale[c], E5M2)
-
-        def flip(c):
-            fgt[c] = k_last_tile("fg")
-            evacuate(transposes(dz1t[c][:].bitcast(F32), 4, "tr"), fgt[c], "ss")
-
-        def weave(c):
-            tgt[c] = interleave_pe(dz1t[c], "acc") if c in VIA_PE else interleave(dz1t[c], "tg", "v")
+        def woven(c):
+            if ("t", c) not in ig:
+                ig["t", c] = keep.tile([P, W, J], BF16, name="tg", tag="tg", align_bytes=64)
+            return ig["t", c]
 
         def weave_g(c):
-            tgt[c] = keep.tile([P, W, J], BF16, name="tg", tag="tg", align_bytes=64)
-            for h0 in range(0, G_COLS, G_STEP):
-                nc.gpsimd.tensor_scalar(
-                    out=tgt[c][:, h0 : h0 + G_STEP, :], in0=dz1t[c][:, :, h0 : h0 + G_STEP].rearrange("p j h -> p h j"),
-                    scalar1=1.0, scalar2=0.0, op0=ALU.mult, op1=ALU.add)
+            woven(c)
+            nc.gpsimd.tensor_scalar(
+                out=ig["t", c][:, 0:G_COLS, :], in0=dz1t[c][:, :, 0:G_COLS].rearrange("p j h -> p h j"),
+                scalar1=1.0, scalar2=0.0, op0=ALU.mult, op1=ALU.add)
 
         def weave_v(c):
-            nc.vector.tensor_copy(out=tgt[c][:, G_COLS:, :], in_=dz1t[c][:, :, G_COLS:].rearrange("p j h -> p h j"))
+            woven(c)
+            nc.vector.tensor_copy(out=ig["t", c][:, G_COLS:, :], in_=dz1t[c][:, :, G_COLS:].rearrange("p j h -> p h j"))
 
-        def weave_x(g):
-            xg[g] = interleave_pe(xt_raw[g], "acc") if XPE else interleave(xt_raw[g], "xg", "s")
+        def weave_p(c, q):
+            bank["t", c, q] = new_bank("acc", [P, 256, J], BF16)
+            for r in range(2):
+                h0 = 256 * q + 128 * r
+                nc.tensor.matmul(
+                    out=bank["t", c, q][:, 128 * r : 128 * (r + 1), :], lhsT=ident_bf[:],
+                    rhs=dz1t[c][:, :, h0 : h0 + 128].rearrange("p j h -> p h j"), start=True, stop=True)
+
+        def take_t(c, q):
+            if ("t", c) not in ig:
+                ig["t", c] = pair.tile([P, W, J], BF16, name="ig", tag="ig", align_bytes=64)
+            nc.scalar.copy(out=ig["t", c][:, 256 * q : 256 * (q + 1), :], in_=bank["t", c, q][:])
+
+        def weave_last(c):
+            ig["t", c] = pair.tile([P, W, J], BF16, name="ig", tag="ig", align_bytes=64)
+            nc.vector.tensor_copy(out=ig["t", c][:], in_=dz1t[c][:].rearrange("p j h -> p h j"))
+
+        def quant_t(c):
+            quantize(ig["t", c][:].rearrange("p w j -> p (w j)"), tq[c], E5M2)
+
+        def weave_x(g, q):
+            bank["x", g, q] = new_bank("acc", [P, 256, J], BF16)
+            for r in range(2):
+                h0 = 256 * q + 128 * r
+                nc.tensor.matmul(
+                    out=bank["x", g, q][:, 128 * r : 128 * (r + 1), :], lhsT=ident_bf[:],
+                    rhs=x_raw[g][:, :, h0 : h0 + 128].rearrange("p j h -> p h j"), start=True, stop=True)
+
+        def take_x(g, q):
+            if ("x", g) not in ig:
+                ig["x", g] = pair.tile([P, W, J], BF16, name="ig", tag="ig", align_bytes=64)
+            nc.scalar.copy(out=ig["x", g][:, 256 * q : 256 * (q + 1), :], in_=bank["x", g, q][:])
 
         def quant_x(g):
-            quantize(flat_t(xg[g]), x_codes[g], x_scale[g], E4M3)
+            quantize(ig["x", g][:].rearrange("p w j -> p (w j)"), xq[g], E4M3)
 
-        wg = {}
+        def copy_out(dst, src, engine):
+            if engine == "s":
+                nc.scalar.copy(out=dst, in_=src)
+            else:
+                nc.vector.tensor_copy(out=dst, in_=src)
 
-        def flip_w(name, raw, tag="acc"):
-            wg[name] = k_last_tile("kg")
-            evacuate(transposes(raw[:].bitcast(F32), 4, tag), wg[name], "ss")
+        def dx(c, j, tag="acc"):
+            bank["dx", c, j] = new_bank(tag)
+            cols = slice(j * P, (j + 1) * P)
+            for hh in range(2):
+                f, w = fq[hh * 4 + c % 4], wq["w1%d" % hh]
+                nc.tensor.matmul_mx(
+                    out=bank["dx", c, j][:], lhsT=f[0][:, cols].bitcast(E5M2), lhsT_scale=f[1][:, cols],
+                    rhs=w[0][:].bitcast(E4M3), rhs_scale=w[1][:], start=(hh == 0), stop=(hh == 1))
 
-        def quant_w(name, codes, scale):
-            quantize(flat4(wg[name]), codes, scale, E4M3)
+        def put_dx(c, j, engine="s"):
+            jj = j // 2
+            if (c, jj) not in outs:
+                outs[c, jj] = trio.tile([P, 2, W], F32, name="dx_out")
+            copy_out(outs[c, jj][:, j % 2, :], bank["dx", c, j][:], engine)
+            if j % 2 == 1:
+                nc.sync.dma_start(out=rows(out_0, c % 4)[:, j - 1 : j + 1, :], in_=outs[c, jj][:])
 
-        def dx_tiles(c, js, tag, engines):
-            for j in js:
-                if j % 2 == 0:
-                    outs[c, j] = trio.tile([P, 2, W], F32, name="dx_out")
-                bank = dx(c, j, tag)
-                copy_out(outs[c, j - j % 2][:, j % 2, :], bank, engines[j % 2])
-                if j % 2 == 1:
-                    store_dx(c, j - 1, j + 1)
+        def dw(i, hh, g, tag="acc"):
+            if g == 0:
+                bank["dw", hh, i] = new_bank(tag)
+            cols = slice(i * P, (i + 1) * P)
+            t = tq[hh * 4 + g]
+            nc.tensor.matmul_mx(
+                out=bank["dw", hh, i][:], lhsT=xq[g][0][:, cols].bitcast(E4M3), lhsT_scale=xq[g][1][:, cols],
+                rhs=t[0][:].bitcast(E5M2), rhs_scale=t[1][:], start=(g == 0), stop=(g == 3))
 
-        dwb = {}
-
-        def dw_all(tiles):
-            for i in tiles:
-                bank = new_bank("acc")
-                for gg in range(GROUPS):
-                    dw_pass(bank, i, 0, gg)
-                store_dw(bank, i, 0, "s")
+        def put_dw(i, hh, engine="s"):
+            t = quad.tile([P, W], F32, name="dw_out")
+            copy_out(t[:], bank["dw", hh, i][:], engine)
+            nc.sync.dma_start(out=out_1[i * P : (i + 1) * P, hh * W : (hh + 1) * W], in_=t[:])
 
         with tc.manual_schedule():
-            load_g(0, 0, 2)
-            load_w2(0)
             load_z1(0, 0, 2)
-            load_g(0, 2, 4)
-            load_z1(0, 2, 4)
-            load_z1(1)
-            load_g(1)
-            load_z1(2)
-            load_w2(1)
-
-            dz2_chain(0, 0, 2)
-            flip_w("w20", w2_raw[0], "tr")
             tanh(0, 0, 2)
-            square(0, 0, 2)
+            load_g(0, 0, 2)
+            load_z1(0, 2, 4)
+            load_g(0, 2, 4)
             side(0, 0, 2)
-            quant_w("w20", w2_codes[0], w2_scale[0])
-            dz2_chain(0, 2, 4)
-            load_g(2)
-            load_z1(3)
-            load_x(0)
-            tanh(0, 2, 4)
-            square(0, 2, 4)
-            slope(0, 0, 2)
+            load_w('w20')
+            load_g(1, 0, 4)
+            mask(0, 0, 2)
             side(0, 2, 4)
-            quant_z(0)
-            tanh(1)
-            for j in range(J):
-                dh(0, j)
-                if j == 2:
-                    slope(0, 2, 4)
-                final(0, j)
-            square(1)
-            flip(0)
-            mask_dz2(1)
-            load_g(3)
-            load_x(1)
-            load_z1(4)
-            side(1)
-            flip_z(1)
-            tanh(2)
-            slope(1)
-            quant_z(1)
-            dh(1, 0)
+            load_z1(1, 0, 4)
+            turn_z(0, 0)
+            square(0, 0, 2)
+            slope(0, 0, 2)
+            mask(0, 2, 4)
+            tanh(0, 2, 4)
+            load_g(2, 0, 4)
+            turn_w('w20', 1, 'tr')
+            take_z(0, 0)
+            load_z1(2, 0, 4)
+            square(0, 2, 4)
+            turn_w('w20', 0, 'tr')
+            slope(0, 2, 4)
+            load_x(0)
+            take_w('w20', 1, 'v')
+            turn_z(0, 1)
+            take_w('w20', 0, 's')
+            quant_z(0, 0, 256)
+            quant_w('w20')
+            take_z(0, 1)
+            load_g(3, 0, 4)
+            dh(0, 1)
+            dh(0, 0)
+            quant_z(0, 256, 512)
+            dh(0, 2)
+            tanh(1, 0, 4)
+            load_w('w10')
+            mask(1, 0, 4)
+            dh(0, 3)
+            turn_z(1, 0)
+            square(1, 0, 4)
+            turn_z(1, 1)
+            final(0, 1)
+            final(0, 0)
+            side(1, 0, 4)
+            take_z(1, 1)
+            final(0, 2)
+            turn_f(0, 0)
+            final(0, 3)
+            take_z(1, 0)
+            mask(2, 0, 4)
+            slope(1, 0, 4)
+            load_z1(3, 0, 4)
+            quant_z(1, 0, 512)
+            weave_p(0, 0)
+            side(2, 0, 4)
+            take_t(0, 0)
+            turn_f(0, 1)
+            tanh(2, 0, 4)
+            turn_z(2, 0)
+            take_z(2, 0)
+            square(2, 0, 4)
+            weave_x(0, 0)
             dh(1, 1)
-            square(2)
-            mask_dz2(2)
-            flip_z(2)
-            side(2)
-            for c in range(1, 8):
-                if c > 1:
-                    quant_t(c - 2)
-                quant_f(c - 1)
-                weave_g(c - 1)
-                if c < 6:
-                    tanh(c + 2)
-                for j in range(J):
-                    if c > 4 and j > 0:
-                        dx_tiles(c - 1, (j - 1,), "acc", "ss")
-                    if j > 1:
-                        dh(c, j)
-                    final(c, j)
-                if c > 4:
-                    dx_tiles(c - 1, (3,), "acc", "ss")
-                if c == 7:
-                    for i in range(4):
-                        dwb[i] = new_bank("acc")
-                        dw_pass(dwb[i], i, 1, 0)
-                        dw_pass(dwb[i], i, 1, 1)
-                flip(c)
-                if c in (2, 3, 4, 5):
-                    quant_x(c - 2)
-                weave_v(c - 1)
-                if c + 1 < 4:
-                    quant_z(c + 1)
-                if c == 3:
-                    quant_w("w21", w2_codes[1], w2_scale[1])
-                if c < 7:
-                    dh(c + 1, 0)
-                    dh(c + 1, 1)
-                if c + 2 < 4:
-                    mask_dz2(c + 2)
-                if c < 7:
-                    slope(c + 1)
-                if c == 5:
-                    dw_all((0, 1))
-                if c == 6:
-                    dw_all((2, 3))
-                if c < 6:
-                    square(c + 2)
-                if c + 2 < 4:
-                    flip_z(c + 2)
-                if c in (3, 4):
-                    quant_w("w1%d" % (c - 3), w1_codes[c - 3], w1_scale[c - 3])
-                if c < 6:
-                    side(c + 2)
-                if c in (1, 2, 3, 4):
-                    weave_x(c - 1)
-                if c + 4 < 8:
-                    load_z1(c + 4)
-                if c == 1:
-                    flip_w("w21", w2_raw[1])
-                    load_x(2)
-                    load_w1(0)
-                if c == 2:
-                    load_x(3)
-                    load_w1(1)
-                if c in (2, 3):
-                    flip_w("w1%d" % (c - 2), w1_raw[c - 2])
-            tgt[7] = interleave(dz1t[7], "tg", "v")
-            quant_t(6)
+            final(1, 1)
+            dh(1, 0)
+            weave_p(0, 1)
+            final(1, 0)
+            mask(3, 0, 4)
+            dh(1, 2)
+            turn_z(2, 1)
+            turn_w('w10', 1, 'acc')
+            take_x(0, 0)
+            weave_x(0, 1)
+            take_z(2, 1)
+            load_w('w21')
+            dh(1, 3)
+            load_w('w11')
+            take_f(0, 1)
+            quant_z(2, 0, 512)
+            take_t(0, 1)
+            slope(2, 0, 4)
+            final(1, 2)
+            turn_w('w10', 0, 'acc')
+            tanh(3, 0, 4)
+            take_f(0, 0)
+            turn_w('w21', 0, 'acc')
+            take_w('w10', 1, 's')
+            quant_t(0)
+            load_z1(4, 0, 4)
+            final(1, 3)
+            turn_f(1, 0)
+            dh(2, 1)
+            dh(2, 0)
+            take_x(0, 1)
+            dh(2, 2)
+            turn_z(3, 0)
+            side(3, 0, 4)
+            square(3, 0, 4)
+            final(2, 1)
+            turn_z(3, 1)
+            turn_w('w21', 1, 'acc')
+            load_x(1)
+            final(2, 0)
+            final(2, 2)
+            take_w('w10', 0, 's')
+            side(4, 0, 4)
+            weave_v(1)
+            slope(3, 0, 4)
+            take_w('w21', 0, 's')
+            turn_w('w11', 0, 'acc')
+            load_z1(6, 0, 4)
+            take_z(3, 0)
+            turn_f(1, 1)
+            dh(2, 3)
+            turn_w('w11', 1, 'acc')
+            final(2, 3)
+            quant_w('w10')
+            take_z(3, 1)
+            take_w('w21', 1, 's')
+            weave_x(1, 0)
+            load_x(3)
+            quant_z(3, 0, 512)
+            load_z1(7, 0, 4)
+            dh(3, 0)
+            weave_g(1)
+            quant_f(0, 0, 512)
+            dh(3, 2)
+            tanh(4, 0, 4)
+            load_z1(5, 0, 4)
+            square(4, 0, 4)
+            take_w('w11', 0, 's')
+            take_f(1, 0)
+            weave_x(1, 1)
+            quant_t(1)
+            take_x(1, 0)
+            take_f(1, 1)
+            weave_g(2)
+            dh(3, 1)
+            load_x(2)
+            dh(3, 3)
+            tanh(5, 0, 4)
+            weave_x(3, 0)
+            turn_f(2, 0)
+            quant_w('w21')
+            turn_f(2, 1)
+            take_w('w11', 1, 's')
+            final(3, 0)
+            final(3, 2)
+            weave_x(2, 0)
+            final(3, 1)
+            dh(4, 0)
+            final(3, 3)
+            dh(4, 2)
+            weave_v(2)
+            weave_x(2, 1)
+            take_f(2, 1)
+            quant_x(0)
+            turn_f(3, 1)
+            slope(4, 0, 4)
+            quant_f(1, 0, 512)
+            quant_t(2)
+            take_x(1, 1)
+            side(5, 0, 4)
+            take_f(2, 0)
+            weave_g(3)
+            final(4, 0)
+            final(4, 2)
+            square(5, 0, 4)
+            weave_x(3, 1)
+            tanh(6, 0, 4)
+            dh(4, 1)
+            final(4, 1)
+            dh(4, 3)
+            final(4, 3)
+            turn_f(4, 0)
+            weave_v(3)
+            quant_w('w11')
+            take_x(2, 0)
+            take_f(3, 1)
+            quant_x(1)
+            turn_f(4, 1)
+            take_f(4, 0)
+            slope(5, 0, 4)
+            take_f(4, 1)
+            dh(5, 0)
+            take_x(3, 0)
+            take_x(2, 1)
+            turn_f(3, 0)
+            quant_f(4, 0, 512)
+            dh(5, 1)
+            take_f(3, 0)
+            dx(4, 0, 'acc')
+            quant_t(3)
+            dx(4, 1, 'acc')
+            square(6, 0, 4)
+            take_x(3, 1)
+            dw(0, 0, 0, 'acc')
+            final(5, 0)
+            dh(5, 3)
+            final(5, 1)
+            dw(0, 0, 1, 'acc')
+            put_dx(4, 0, 's')
+            final(5, 3)
+            dh(5, 2)
+            final(5, 2)
+            dx(4, 2, 'acc')
+            dw(1, 0, 0, 'acc')
+            turn_f(5, 0)
+            side(6, 0, 4)
+            put_dx(4, 2, 's')
+            put_dx(4, 1, 's')
+            turn_f(5, 1)
+            quant_x(2)
+            take_f(5, 1)
+            quant_x(3)
+            weave_g(4)
+            dw(0, 0, 2, 'acc')
+            dx(4, 3, 'acc')
+            dw(0, 0, 3, 'acc')
+            take_f(5, 0)
+            dw(1, 0, 1, 'acc')
+            dw(1, 0, 2, 'acc')
+            weave_v(4)
+            dh(6, 0)
+            slope(6, 0, 4)
+            dw(1, 0, 3, 'acc')
+            quant_f(5, 0, 512)
+            dh(6, 2)
+            quant_t(4)
+            dx(5, 2, 'acc')
+            dx(5, 0, 'acc')
+            final(6, 0)
+            put_dw(0, 0, 's')
+            final(6, 2)
+            tanh(7, 0, 4)
+            dh(6, 3)
+            dh(6, 1)
+            dx(5, 1, 'acc')
+            final(6, 3)
+            dx(5, 3, 'acc')
+            weave_g(5)
+            dw(2, 0, 0, 'acc')
+            dh(7, 0)
+            final(6, 1)
+            weave_g(6)
+            put_dw(1, 0, 's')
+            put_dx(5, 0, 's')
+            dh(7, 3)
+            dw(3, 0, 0, 'acc')
+            put_dx(4, 3, 's')
+            turn_f(6, 1)
+            turn_f(6, 0)
+            put_dx(5, 2, 's')
+            dw(2, 0, 1, 'acc')
+            square(7, 0, 4)
+            put_dx(5, 1, 's')
+            dw(3, 0, 1, 'acc')
+            take_f(6, 1)
+            take_f(6, 0)
+            side(7, 0, 4)
+            weave_v(5)
+            dw(1, 1, 0, 'acc')
+            quant_f(2, 0, 512)
+            slope(7, 0, 4)
+            quant_f(6, 0, 512)
+            final(7, 0)
+            dw(3, 0, 2, 'acc')
+            dw(2, 0, 2, 'acc')
+            dw(2, 0, 3, 'acc')
+            quant_t(5)
+            put_dx(5, 3, 's')
+            dw(2, 1, 0, 'acc')
+            final(7, 3)
+            dx(6, 2, 'tr')
+            dx(6, 0, 'tr')
+            put_dx(6, 2, 's')
+            dh(7, 2)
+            dx(6, 1, 'tr')
+            dh(7, 1)
+            dw(3, 0, 3, 'acc')
+            dx(6, 3, 'tr')
+            dw(3, 1, 0, 'acc')
+            dw(1, 1, 1, 'acc')
+            final(7, 2)
+            put_dw(2, 0, 's')
+            dw(2, 1, 1, 'acc')
+            put_dx(6, 0, 's')
+            put_dw(3, 0, 's')
+            dw(0, 1, 0, 'acc')
+            final(7, 1)
+            quant_f(3, 0, 512)
+            weave_v(6)
+            weave_last(7)
+            put_dx(6, 1, 's')
+            put_dx(6, 3, 's')
+            turn_f(7, 0)
+            turn_f(7, 1)
+            take_f(7, 0)
+            dw(0, 1, 1, 'acc')
             quant_f(7, 0, 256)
+            quant_t(6)
+            take_f(7, 1)
+            dx(7, 0, 'tr')
+            dx(7, 1, 'tr')
+            dw(0, 1, 2, 'acc')
+            dw(1, 1, 2, 'acc')
             quant_t(7)
+            dw(2, 1, 2, 'acc')
+            dw(0, 1, 3, 'acc')
+            dw(3, 1, 1, 'acc')
+            dw(2, 1, 3, 'acc')
+            dw(1, 1, 3, 'acc')
+            dw(3, 1, 2, 'acc')
+            put_dx(7, 0, 'v')
             quant_f(7, 256, 512)
-            for i in range(4):
-                dw_pass(dwb[i], i, 1, 2)
-            dx_tiles(7, (0, 1), "tr", "vs")
-            for i in range(4):
-                dw_pass(dwb[i], i, 1, 3)
-                store_dw(dwb[i], i, 1, "vs"[i % 2])
-            dx_tiles(7, (2, 3), "dhb", "vs")
+            put_dx(7, 1, 's')
+            put_dw(0, 1, 'v')
+            dw(3, 1, 3, 'acc')
+            put_dw(2, 1, 'v')
+            put_dw(1, 1, 's')
+            dx(7, 3, 'dhb')
+            dx(7, 2, 'dhb')
+            put_dx(7, 2, 'v')
+            put_dw(3, 1, 's')
+            put_dx(7, 3, 's')

import math
from contextlib import ExitStack

import concourse.mybir as mybir
from concourse.masks import make_identity

FLOPS = 3 * 2 * 2048 * 512 * 1024
BYTES = 2048 * 512 * 2 * 2 + 512 * 1024 * 2 * 2 + 2048 * 1024 * 4 + 2048 * 512 * 4 + 2048 * 512 * 4 + 512 * 1024 * 4

F32 = mybir.dt.float32
BF16 = mybir.dt.bfloat16
U32 = mybir.dt.uint32
U8 = mybir.dt.uint8
E4M3 = mybir.dt.float8_e4m3fn_x4
E5M2 = mybir.dt.float8_e5m2_x4
ALU = mybir.AluOpType
ACT = mybir.ActivationFunctionType

P = 128
J = 4
W = 512
C_SQ = math.sqrt(0.4)
G_COLS = 352
BANKS = {"tr": 2, "acc": 4, "dhb": 2}


def tile_complexnn_pa_v_kernel(tc, x, W1, b1, W2, b2, z1, z2, grad_out, out_0, out_1):
    nc = tc.nc
    with ExitStack() as ctx:
        keep = ctx.enter_context(tc.tile_pool(name="keep", bufs=1))
        zin = ctx.enter_context(tc.tile_pool(name="zin", bufs=4))
        pair = ctx.enter_context(tc.tile_pool(name="pair", bufs=2))
        trio = ctx.enter_context(tc.tile_pool(name="trio", bufs=3))
        quad = ctx.enter_context(tc.tile_pool(name="quad", bufs=4))
        psum = ctx.enter_context(tc.psum_pool(name="psum", bufs=2))

        ident = keep.tile([P, P], F32, name="ident")
        make_identity(nc, ident[:])
        ident_bf = keep.tile([P, P], BF16, name="ident_bf")
        nc.vector.tensor_copy(out=ident_bf[:], in_=ident[:])
        warm = keep.tile([P, 8], F32, name="warm")
        nc.vector.memset(warm[:], 0.0)
        warm_out = keep.tile([P, 8], F32, name="warm_out")
        nc.scalar.activation(out=warm_out[:], in_=warm[:], func=ACT.Tanh)

        def codes_pair(name):
            return (keep.tile([P, W], U32, name="c_" + name, align_bytes=64), keep.tile([P, W], U8, name="s_" + name, align_bytes=64))

        wq = {n: codes_pair(n) for n in ("w20", "w21", "w10", "w11")}
        zq = [codes_pair("z%d" % g) for g in range(4)]
        xq = [codes_pair("x%d" % g) for g in range(4)]
        tq = [codes_pair("t%d" % c) for c in range(8)]
        fq = {c: codes_pair("f%d" % c) for c in range(4)}
        bank, z1t, z2t, gt, x_raw, w_raw, kg, ig, tt, nt, dz1t, outs = {}, {}, {}, {}, {}, {}, {}, {}, {}, {}, {}, {}

        def rows(dram, g):
            return dram[g * W : (g + 1) * W, :].rearrange("(p j) w -> p j w", j=J)

        def new_bank(tag, shape=(P, W), dtype=F32):
            return psum.tile(list(shape), dtype, name=tag, tag=tag, bufs=BANKS[tag])

        def load_z1(c, j0=0, j1=J):
            if c not in z1t:
                z1t[c] = zin.tile([P, J, W], F32, name="z1c")
            h0 = (c // 4) * W
            nc.sync.dma_start(out=z1t[c][:, j0:j1, :], in_=rows(z1, c % 4)[:, j0:j1, h0 : h0 + W])

        def load_g(g, j0=0, j1=J):
            if g not in z2t:
                z2t[g] = pair.tile([P, J, W], F32, name="z2g")
                gt[g] = trio.tile([P, J, W], BF16, name="gg")
            nc.sync.dma_start(out=z2t[g][:, j0:j1, :], in_=rows(z2, g)[:, j0:j1, :])
            nc.sync.dma_start(out=gt[g][:, j0:j1, :], in_=rows(grad_out, g)[:, j0:j1, :])

        def load_w(n):
            w_raw[n] = pair.tile([P, 4, W], BF16, name="w_raw", tag="w_raw")
            h0 = int(n[2]) * W
            src = W2[h0 : h0 + W, :] if n[1] == "2" else W1[:, h0 : h0 + W]
            nc.sync.dma_start(out=w_raw[n][:], in_=src.rearrange("(i p) f -> p i f", p=P))

        def load_x(g):
            x_raw[g] = pair.tile([P, J, W], BF16, name="x_raw")
            nc.sync.dma_start(out=x_raw[g][:], in_=rows(x, g))

        def turn(key, src, q, tag):
            bank[key, q] = new_bank(tag, [P, 2, 2, P])
            words = src[:].bitcast(F32)
            for b in range(2):
                for u in range(2):
                    nc.tensor.transpose(bank[key, q][:, b, u, :], words[:, 2 * q + b, u:256:2], ident[:])

        def take(key, q, engine="s"):
            if key not in kg:
                kg[key] = quad.tile([P, 4, P, 4], BF16, name="kg", tag="kg", align_bytes=64)
            out = kg[key][:].bitcast(F32)[:, 2 * q : 2 * q + 2, :, :]
            in_ = bank[key, q][:].rearrange("p b u r -> p b r u")
            if engine == "s":
                nc.scalar.copy(out=out, in_=in_)
            else:
                nc.vector.tensor_copy(out=out, in_=in_)

        def quantize(flat, dst, fmt, c0=0, c1=W):
            nc.vector.quantize_mx(out=dst[0][:, c0:c1].bitcast(fmt), scales=dst[1][:, c0:c1], in_=flat[:, 4 * c0 : 4 * c1])

        def flat_k(key):
            return kg[key][:].rearrange("p b r k -> p (b r k)")

        def turn_w(n, q, tag="acc"):
            turn(n, w_raw[n], q, tag)

        def take_w(n, q, engine="s"):
            take(n, q, engine)

        def quant_w(n):
            quantize(flat_k(n), wq[n], E4M3)

        def mask(g, j0=0, j1=J):
            nc.vector.scalar_tensor_tensor(
                out=gt[g][:, j0:j1, :], in0=z2t[g][:, j0:j1, :], scalar=0.0, in1=gt[g][:, j0:j1, :], op0=ALU.is_gt, op1=ALU.mult)

        def turn_z(g, q):
            turn(("z", g), gt[g], q, "acc")

        def take_z(g, q):
            take(("z", g), q)

        def quant_z(g, c0=0, c1=W):
            quantize(flat_k(("z", g)), zq[g], E5M2, c0, c1)

        def tanh(c, j0=0, j1=J):
            if c not in tt:
                tt[c] = trio.tile([P, J, W], F32, name="th")
            nc.scalar.activation(out=tt[c][:, j0:j1, :], in_=z1t[c][:, j0:j1, :], func=ACT.Tanh)

        def square(c, j0=0, j1=J):
            nc.scalar.activation(out=tt[c][:, j0:j1, :], in_=tt[c][:, j0:j1, :], func=ACT.Square, scale=C_SQ)

        def side(c, j0=0, j1=J):
            if c not in nt:
                nt[c] = pair.tile([P, J, W], BF16, name="side")
            nc.vector.tensor_scalar(
                out=nt[c][:, j0:j1, :], in0=z1t[c][:, j0:j1, :], scalar1=0.0, scalar2=1.25, op0=ALU.is_gt, op1=ALU.subtract)

        def slope(c, j0=0, j1=J):
            nc.vector.scalar_tensor_tensor(
                out=tt[c][:, j0:j1, :], in0=tt[c][:, j0:j1, :], scalar=0.5, in1=nt[c][:, j0:j1, :], op0=ALU.add, op1=ALU.mult)

        def dh(c, j):
            bank["dh", c, j] = new_bank("dhb")
            z, w = zq[c % 4], wq["w2%d" % (c // 4)]
            cols = slice(j * P, (j + 1) * P)
            nc.tensor.matmul_mx(
                out=bank["dh", c, j][:], lhsT=z[0][:, cols].bitcast(E5M2), lhsT_scale=z[1][:, cols],
                rhs=w[0][:].bitcast(E4M3), rhs_scale=w[1][:], start=True, stop=True)

        def final(c, j):
            if c not in dz1t:
                dz1t[c] = pair.tile([P, J, W], BF16, name="dz1")
            nc.vector.scalar_tensor_tensor(
                out=dz1t[c][:, j, :], in0=tt[c][:, j, :], scalar=1.125, in1=bank["dh", c, j][:], op0=ALU.add, op1=ALU.mult)

        def turn_f(c, q):
            turn(("f", c), dz1t[c], q, "tr")

        def take_f(c, q):
            take(("f", c), q)

        def quant_f(c, c0=0, c1=W):
            if c not in fq:
                fq[c] = (pair.tile([P, W], U32, name="c_f", align_bytes=64), pair.tile([P, W], U8, name="s_f", align_bytes=64))
            quantize(flat_k(("f", c)), fq[c], E5M2, c0, c1)

        def woven(c):
            if ("t", c) not in ig:
                ig["t", c] = keep.tile([P, W, J], BF16, name="tg", tag="tg", align_bytes=64)
            return ig["t", c]

        def weave_g(c):
            woven(c)
            nc.gpsimd.tensor_scalar(
                out=ig["t", c][:, 0:G_COLS, :], in0=dz1t[c][:, :, 0:G_COLS].rearrange("p j h -> p h j"),
                scalar1=1.0, scalar2=0.0, op0=ALU.mult, op1=ALU.add)

        def weave_v(c):
            woven(c)
            nc.vector.tensor_copy(out=ig["t", c][:, G_COLS:, :], in_=dz1t[c][:, :, G_COLS:].rearrange("p j h -> p h j"))

        def weave_p(c, q):
            bank["t", c, q] = new_bank("acc", [P, 256, J], BF16)
            for r in range(2):
                h0 = 256 * q + 128 * r
                nc.tensor.matmul(
                    out=bank["t", c, q][:, 128 * r : 128 * (r + 1), :], lhsT=ident_bf[:],
                    rhs=dz1t[c][:, :, h0 : h0 + 128].rearrange("p j h -> p h j"), start=True, stop=True)

        def take_t(c, q):
            if ("t", c) not in ig:
                ig["t", c] = pair.tile([P, W, J], BF16, name="ig", tag="ig", align_bytes=64)
            nc.scalar.copy(out=ig["t", c][:, 256 * q : 256 * (q + 1), :], in_=bank["t", c, q][:])

        def weave_last(c):
            ig["t", c] = pair.tile([P, W, J], BF16, name="ig", tag="ig", align_bytes=64)
            nc.vector.tensor_copy(out=ig["t", c][:], in_=dz1t[c][:].rearrange("p j h -> p h j"))

        def quant_t(c):
            quantize(ig["t", c][:].rearrange("p w j -> p (w j)"), tq[c], E5M2)

        def weave_x(g, q):
            bank["x", g, q] = new_bank("acc", [P, 256, J], BF16)
            for r in range(2):
                h0 = 256 * q + 128 * r
                nc.tensor.matmul(
                    out=bank["x", g, q][:, 128 * r : 128 * (r + 1), :], lhsT=ident_bf[:],
                    rhs=x_raw[g][:, :, h0 : h0 + 128].rearrange("p j h -> p h j"), start=True, stop=True)

        def take_x(g, q):
            if ("x", g) not in ig:
                ig["x", g] = pair.tile([P, W, J], BF16, name="ig", tag="ig", align_bytes=64)
            nc.scalar.copy(out=ig["x", g][:, 256 * q : 256 * (q + 1), :], in_=bank["x", g, q][:])

        def quant_x(g):
            quantize(ig["x", g][:].rearrange("p w j -> p (w j)"), xq[g], E4M3)

        def copy_out(dst, src, engine):
            if engine == "s":
                nc.scalar.copy(out=dst, in_=src)
            else:
                nc.vector.tensor_copy(out=dst, in_=src)

        def dx(c, j, tag="acc"):
            bank["dx", c, j] = new_bank(tag)
            cols = slice(j * P, (j + 1) * P)
            for hh in range(2):
                f, w = fq[hh * 4 + c % 4], wq["w1%d" % hh]
                nc.tensor.matmul_mx(
                    out=bank["dx", c, j][:], lhsT=f[0][:, cols].bitcast(E5M2), lhsT_scale=f[1][:, cols],
                    rhs=w[0][:].bitcast(E4M3), rhs_scale=w[1][:], start=(hh == 0), stop=(hh == 1))

        def put_dx(c, j, engine="s"):
            jj = j // 2
            if (c, jj) not in outs:
                outs[c, jj] = trio.tile([P, 2, W], F32, name="dx_out")
            copy_out(outs[c, jj][:, j % 2, :], bank["dx", c, j][:], engine)
            if j % 2 == 1:
                nc.sync.dma_start(out=rows(out_0, c % 4)[:, j - 1 : j + 1, :], in_=outs[c, jj][:])

        def dw(i, hh, g, tag="acc"):
            if g == 0:
                bank["dw", hh, i] = new_bank(tag)
            cols = slice(i * P, (i + 1) * P)
            t = tq[hh * 4 + g]
            nc.tensor.matmul_mx(
                out=bank["dw", hh, i][:], lhsT=xq[g][0][:, cols].bitcast(E4M3), lhsT_scale=xq[g][1][:, cols],
                rhs=t[0][:].bitcast(E5M2), rhs_scale=t[1][:], start=(g == 0), stop=(g == 3))

        def put_dw(i, hh, engine="s"):
            t = quad.tile([P, W], F32, name="dw_out")
            copy_out(t[:], bank["dw", hh, i][:], engine)
            nc.sync.dma_start(out=out_1[i * P : (i + 1) * P, hh * W : (hh + 1) * W], in_=t[:])

        with tc.manual_schedule():
            load_z1(0, 0, 2)
            tanh(0, 0, 2)
            load_g(0, 0, 2)
            load_z1(0, 2, 4)
            load_g(0, 2, 4)
            side(0, 0, 2)
            load_w('w20')
            load_g(1, 0, 4)
            mask(0, 0, 2)
            side(0, 2, 4)
            load_z1(1, 0, 4)
            turn_z(0, 0)
            square(0, 0, 2)
            slope(0, 0, 2)
            mask(0, 2, 4)
            tanh(0, 2, 4)
            load_g(2, 0, 4)
            turn_w('w20', 1, 'tr')
            take_z(0, 0)
            load_z1(2, 0, 4)
            square(0, 2, 4)
            turn_w('w20', 0, 'tr')
            slope(0, 2, 4)
            load_x(0)
            take_w('w20', 1, 'v')
            turn_z(0, 1)
            take_w('w20', 0, 's')
            quant_z(0, 0, 256)
            quant_w('w20')
            take_z(0, 1)
            load_g(3, 0, 4)
            dh(0, 1)
            dh(0, 0)
            quant_z(0, 256, 512)
            dh(0, 2)
            tanh(1, 0, 4)
            load_w('w10')
            mask(1, 0, 4)
            dh(0, 3)
            turn_z(1, 0)
            square(1, 0, 4)
            turn_z(1, 1)
            final(0, 1)
            final(0, 0)
            side(1, 0, 4)
            take_z(1, 1)
            final(0, 2)
            turn_f(0, 0)
            final(0, 3)
            take_z(1, 0)
            mask(2, 0, 4)
            slope(1, 0, 4)
            load_z1(3, 0, 4)
            quant_z(1, 0, 512)
            weave_p(0, 0)
            side(2, 0, 4)
            take_t(0, 0)
            turn_f(0, 1)
            tanh(2, 0, 4)
            turn_z(2, 0)
            take_z(2, 0)
            square(2, 0, 4)
            weave_x(0, 0)
            dh(1, 1)
            final(1, 1)
            dh(1, 0)
            weave_p(0, 1)
            final(1, 0)
            mask(3, 0, 4)
            dh(1, 2)
            turn_z(2, 1)
            turn_w('w10', 1, 'acc')
            take_x(0, 0)
            weave_x(0, 1)
            take_z(2, 1)
            load_w('w21')
            dh(1, 3)
            load_w('w11')
            take_f(0, 1)
            quant_z(2, 0, 512)
            take_t(0, 1)
            slope(2, 0, 4)
            final(1, 2)
            turn_w('w10', 0, 'acc')
            tanh(3, 0, 4)
            take_f(0, 0)
            turn_w('w21', 0, 'acc')
            take_w('w10', 1, 's')
            quant_t(0)
            load_z1(4, 0, 4)
            final(1, 3)
            turn_f(1, 0)
            dh(2, 1)
            dh(2, 0)
            take_x(0, 1)
            dh(2, 2)
            turn_z(3, 0)
            side(3, 0, 4)
            square(3, 0, 4)
            final(2, 1)
            turn_z(3, 1)
            turn_w('w21', 1, 'acc')
            load_x(1)
            final(2, 0)
            final(2, 2)
            take_w('w10', 0, 's')
            side(4, 0, 4)
            weave_v(1)
            slope(3, 0, 4)
            take_w('w21', 0, 's')
            turn_w('w11', 0, 'acc')
            load_z1(6, 0, 4)
            take_z(3, 0)
            turn_f(1, 1)
            dh(2, 3)
            turn_w('w11', 1, 'acc')
            final(2, 3)
            quant_w('w10')
            take_z(3, 1)
            take_w('w21', 1, 's')
            weave_x(1, 0)
            load_x(3)
            quant_z(3, 0, 512)
            load_z1(7, 0, 4)
            dh(3, 0)
            weave_g(1)
            quant_f(0, 0, 512)
            dh(3, 2)
            tanh(4, 0, 4)
            load_z1(5, 0, 4)
            square(4, 0, 4)
            take_w('w11', 0, 's')
            take_f(1, 0)
            weave_x(1, 1)
            quant_t(1)
            take_x(1, 0)
            take_f(1, 1)
            weave_g(2)
            dh(3, 1)
            load_x(2)
            dh(3, 3)
            tanh(5, 0, 4)
            weave_x(3, 0)
            turn_f(2, 0)
            quant_w('w21')
            turn_f(2, 1)
            take_w('w11', 1, 's')
            final(3, 0)
            final(3, 2)
            weave_x(2, 0)
            final(3, 1)
            dh(4, 0)
            final(3, 3)
            dh(4, 2)
            weave_v(2)
            weave_x(2, 1)
            take_f(2, 1)
            quant_x(0)
            turn_f(3, 1)
            slope(4, 0, 4)
            quant_f(1, 0, 512)
            quant_t(2)
            take_x(1, 1)
            side(5, 0, 4)
            take_f(2, 0)
            weave_g(3)
            final(4, 0)
            final(4, 2)
            square(5, 0, 4)
            weave_x(3, 1)
            tanh(6, 0, 4)
            dh(4, 1)
            final(4, 1)
            dh(4, 3)
            final(4, 3)
            turn_f(4, 0)
            weave_v(3)
            quant_w('w11')
            take_x(2, 0)
            take_f(3, 1)
            quant_x(1)
            turn_f(4, 1)
            take_f(4, 0)
            slope(5, 0, 4)
            take_f(4, 1)
            dh(5, 0)
            take_x(3, 0)
            take_x(2, 1)
            turn_f(3, 0)
            quant_f(4, 0, 512)
            dh(5, 1)
            take_f(3, 0)
            dx(4, 0, 'acc')
            quant_t(3)
            dx(4, 1, 'acc')
            square(6, 0, 4)
            take_x(3, 1)
            dw(0, 0, 0, 'acc')
            final(5, 0)
            dh(5, 3)
            final(5, 1)
            dw(0, 0, 1, 'acc')
            put_dx(4, 0, 's')
            final(5, 3)
            dh(5, 2)
            final(5, 2)
            dx(4, 2, 'acc')
            dw(1, 0, 0, 'acc')
            turn_f(5, 0)
            side(6, 0, 4)
            put_dx(4, 2, 's')
            put_dx(4, 1, 's')
            turn_f(5, 1)
            quant_x(2)
            take_f(5, 1)
            quant_x(3)
            weave_g(4)
            dw(0, 0, 2, 'acc')
            dx(4, 3, 'acc')
            dw(0, 0, 3, 'acc')
            take_f(5, 0)
            dw(1, 0, 1, 'acc')
            dw(1, 0, 2, 'acc')
            weave_v(4)
            dh(6, 0)
            slope(6, 0, 4)
            dw(1, 0, 3, 'acc')
            quant_f(5, 0, 512)
            dh(6, 2)
            quant_t(4)
            dx(5, 2, 'acc')
            dx(5, 0, 'acc')
            final(6, 0)
            put_dw(0, 0, 's')
            final(6, 2)
            tanh(7, 0, 4)
            dh(6, 3)
            dh(6, 1)
            dx(5, 1, 'acc')
            final(6, 3)
            dx(5, 3, 'acc')
            weave_g(5)
            dw(2, 0, 0, 'acc')
            dh(7, 0)
            final(6, 1)
            weave_g(6)
            put_dw(1, 0, 's')
            put_dx(5, 0, 's')
            dh(7, 3)
            dw(3, 0, 0, 'acc')
            put_dx(4, 3, 's')
            turn_f(6, 1)
            turn_f(6, 0)
            put_dx(5, 2, 's')
            dw(2, 0, 1, 'acc')
            square(7, 0, 4)
            put_dx(5, 1, 's')
            dw(3, 0, 1, 'acc')
            take_f(6, 1)
            take_f(6, 0)
            side(7, 0, 4)
            weave_v(5)
            dw(1, 1, 0, 'acc')
            quant_f(2, 0, 512)
            slope(7, 0, 4)
            quant_f(6, 0, 512)
            final(7, 0)
            dw(3, 0, 2, 'acc')
            dw(2, 0, 2, 'acc')
            dw(2, 0, 3, 'acc')
            quant_t(5)
            put_dx(5, 3, 's')
            dw(2, 1, 0, 'acc')
            final(7, 3)
            dx(6, 2, 'tr')
            dx(6, 0, 'tr')
            put_dx(6, 2, 's')
            dh(7, 2)
            dx(6, 1, 'tr')
            dh(7, 1)
            dw(3, 0, 3, 'acc')
            dx(6, 3, 'tr')
            dw(3, 1, 0, 'acc')
            dw(1, 1, 1, 'acc')
            final(7, 2)
            put_dw(2, 0, 's')
            dw(2, 1, 1, 'acc')
            put_dx(6, 0, 's')
            put_dw(3, 0, 's')
            dw(0, 1, 0, 'acc')
            final(7, 1)
            quant_f(3, 0, 512)
            weave_v(6)
            weave_last(7)
            put_dx(6, 1, 's')
            put_dx(6, 3, 's')
            turn_f(7, 0)
            turn_f(7, 1)
            take_f(7, 0)
            dw(0, 1, 1, 'acc')
            quant_f(7, 0, 256)
            quant_t(6)
            take_f(7, 1)
            dx(7, 0, 'tr')
            dx(7, 1, 'tr')
            dw(0, 1, 2, 'acc')
            dw(1, 1, 2, 'acc')
            quant_t(7)
            dw(2, 1, 2, 'acc')
            dw(0, 1, 3, 'acc')
            dw(3, 1, 1, 'acc')
            dw(2, 1, 3, 'acc')
            dw(1, 1, 3, 'acc')
            dw(3, 1, 2, 'acc')
            put_dx(7, 0, 'v')
            quant_f(7, 256, 512)
            put_dx(7, 1, 's')
            put_dw(0, 1, 'v')
            dw(3, 1, 3, 'acc')
            put_dw(2, 1, 'v')
            put_dw(1, 1, 's')
            dx(7, 3, 'dhb')
            dx(7, 2, 'dhb')
            put_dx(7, 2, 'v')
            put_dw(3, 1, 's')
            put_dx(7, 3, 's')
